import numpy as np
import ml_dtypes


def mxq(x, axis, fmt="e4m3"):
    dtype, down = {"e4m3": (ml_dtypes.float8_e4m3fn, 7), "e5m2": (ml_dtypes.float8_e5m2, 14)}[fmt]
    v = np.moveaxis(np.asarray(x, np.float32).astype(ml_dtypes.bfloat16).astype(np.float64), axis, -1)
    blocks = v.reshape(v.shape[:-1] + (-1, 32))
    amax = np.abs(blocks).max(-1, keepdims=True)
    byte = np.maximum(np.where(amax > 0, np.frexp(amax)[1] - 1 + 127, 0) - down, 1)
    scale = np.exp2(byte - 127.0)
    codes = (blocks / scale).astype(np.float32).astype(dtype).astype(np.float64)
    return np.moveaxis((codes * scale).reshape(v.shape), -1, axis)


WIDE = False


def mx_kscale(k):
    if not WIDE:
        return np.ones(k)
    levels = np.array([10, -10, 5, -5, 0])
    a = np.random.permutation(np.resize(levels, k // 512 * 4)).reshape(k // 512, 4)
    idx = np.arange(k)
    return np.exp2(a[idx // 512, idx % 128 // 32])


BF16 = ml_dtypes.bfloat16


def bf(x):
    return np.asarray(x, np.float32).astype(BF16)


def f64(x):
    return np.asarray(x).astype(np.float64)


E2M1 = np.array([0.0, 0.5, 1.0, 1.5, 2.0, 3.0, 4.0, 6.0, -0.0, -0.5, -1.0, -1.5, -2.0, -3.0, -4.0, -6.0])


def pack_weight(w, fmt):
    k, n = w.shape
    w = f64(bf(w)).reshape(k // 32, 32, n)
    amax = np.abs(w).max(1)
    if fmt == "e4m3":
        byte = np.frexp(amax)[1] - 1 + 127 - 7
    else:
        mant, ex = np.frexp(amax / 6.0)
        byte = np.where(mant > 0.5, ex, ex - 1) + 127
    byte = np.clip(np.where(amax > 0, byte, 1), 1, 254)
    scaled = (w * np.exp2(127.0 - byte)[:, None, :]).reshape(k, n).astype(np.float32)
    by_word = np.ascontiguousarray(scaled.reshape(k // 512, 128, 4, n).transpose(0, 1, 3, 2))
    if fmt == "e4m3":
        words = by_word.astype(ml_dtypes.float8_e4m3fn).view(np.uint8)
    else:
        c = by_word.astype(ml_dtypes.float4_e2m1fn).view(np.uint8) & 0xF
        words = c[..., 0::2] | (c[..., 1::2] << 4)
    return np.ascontiguousarray(words), np.ascontiguousarray(byte.astype(np.uint8).reshape(k // 512, 16, n))


def unpack_weight(words, scales, fmt):
    g, p, n, _ = words.shape
    if fmt == "e4m3":
        vals = np.ascontiguousarray(words).view(ml_dtypes.float8_e4m3fn).astype(np.float64)
    else:
        nib = np.empty((g, p, n, 4), np.uint8)
        nib[..., 0::2] = words & 0xF
        nib[..., 1::2] = words >> 4
        vals = E2M1[nib]
    vals = vals * np.repeat(np.exp2(scales.astype(np.float64) - 127.0), 8, axis=1)[..., None]
    return vals.transpose(0, 1, 3, 2).reshape(g * 512, n)


B, C_IN, H, W, HID, K, C_OUT = 2, 1024, 32, 32, 128, 8, 256


def setup_inputs():
    s = mx_kscale(C_IN)
    x = bf(np.random.standard_normal((B, C_IN, H, W)) * s[None, :, None, None])
    w_in = np.random.standard_normal((HID, C_IN)) / np.sqrt(C_IN) / s[None, :]
    w_in_words, w_in_scales = pack_weight(np.ascontiguousarray(w_in.T), "e4m3")
    return {
        "x": x,
        "w_in_words": w_in_words,
        "w_in_scales": w_in_scales,
        "b_in": bf(np.random.standard_normal(HID) * 0.3),
        "centers": bf(np.linspace(-2.0, 2.0, K).reshape(1, 1, K, 1, 1) + 0.1 * np.random.standard_normal((1, HID, K, 1, 1))),
        "log_widths": bf(np.random.standard_normal((1, HID, K, 1, 1)) * 0.3),
        "out_weight": bf(np.random.standard_normal((C_OUT, HID, K)) * 2.0 / np.sqrt(HID * K)),
        "out_bias": bf(np.random.standard_normal(C_OUT) * 0.3),
    }


def reference(x, w_in_words, w_in_scales, b_in, centers, log_widths, out_weight, out_bias):
    xq = mxq(f64(x), 1, "e4m3")
    z = (unpack_weight(w_in_words, w_in_scales, "e4m3").T @ xq.reshape(B, C_IN, H * W)).reshape(B, HID, H, W) + f64(b_in)[None, :, None, None]
    z = z[:, :, None, :, :]
    widths = np.logaddexp(f64(log_widths), 0.0) + 1e-4
    phi = np.exp(-(((z - f64(centers)) / widths) ** 2))
    pq = mxq(phi.reshape(B, HID * K, H * W), 1, "e4m3")
    out = (mxq(f64(out_weight).reshape(C_OUT, HID * K), 1, "e4m3") @ pq).reshape(B, C_OUT, H, W)
    return out + f64(out_bias)[None, :, None, None]

@@ -1,0 +1,220 @@
+from contextlib import ExitStack
+
+import concourse.mybir as mybir
+from concourse.masks import make_identity
+
+F32 = mybir.dt.float32
+BF16 = mybir.dt.bfloat16
+I32 = mybir.dt.int32
+U32 = mybir.dt.uint32
+U8 = mybir.dt.uint8
+FP8X4 = mybir.dt.float8_e4m3fn_x4
+ACT = mybir.ActivationFunctionType
+ALU = mybir.AluOpType
+
+B, C_IN, HW, HID, K, C_OUT = 2, 1024, 32 * 32, 128, 8, 256
+P = 128
+PACK = 4
+K_PASS = P * PACK
+IN_PASSES = C_IN // K_PASS
+RBF_PASSES = HID * K // K_PASS
+O_TILES = C_OUT // P
+PIX = 512
+CHUNKS_PER_IMAGE = HW // PIX
+RUN = 4
+K_ON_SCALAR = 6
+
+FLOPS = 2 * B * HW * C_IN * HID + 2 * B * HW * HID * K * C_OUT
+
+
+def tile_rbfkanhead_kernel(
+    tc, x, w_in_words, w_in_scales, b_in, centers, log_widths, out_weight, out_bias, out
+):
+    nc = tc.nc
+    with ExitStack() as ctx:
+        consts = ctx.enter_context(tc.tile_pool(name="consts", bufs=1))
+        x_pool = ctx.enter_context(tc.tile_pool(name="x_pool", bufs=B * CHUNKS_PER_IMAGE))
+        work = ctx.enter_context(tc.tile_pool(name="work", bufs=2))
+        stores = ctx.enter_context(tc.tile_pool(name="stores", bufs=4))
+        z_banks = ctx.enter_context(tc.psum_pool(name="z_banks", bufs=2))
+        out_banks = ctx.enter_context(tc.psum_pool(name="out_banks", bufs=4))
+
+        def load_x(chunk):
+            image = x[chunk // CHUNKS_PER_IMAGE].rearrange("(g p t) h w -> g p t (h w)", p=P, t=PACK)
+            first = (chunk % CHUNKS_PER_IMAGE) * PIX
+            x_raw = x_pool.tile([P, IN_PASSES, PACK, PIX], BF16, name="x_raw")
+            for g in range(IN_PASSES):
+                nc.sync.dma_start(out=x_raw[:, g], in_=image[g, :, :, first : first + PIX])
+            return x_raw
+
+        lw_bf = consts.tile([P, K], BF16)
+        nc.scalar.dma_start(out=lw_bf[:], in_=log_widths[0, :, :, 0, 0])
+        centers_bf = consts.tile([P, K], BF16)
+        nc.scalar.dma_start(out=centers_bf[:], in_=centers[0, :, :, 0, 0])
+        b_in_bf = consts.tile([P, 1], BF16)
+        nc.scalar.dma_start(out=b_in_bf[:], in_=b_in.rearrange("(c one) -> c one", one=1))
+        out_bias_bf = []
+        for a in range(O_TILES):
+            bias_bf = consts.tile([P, 1], BF16, name="out_bias_bf%d" % a)
+            nc.scalar.dma_start(
+                out=bias_bf[:], in_=out_bias[a * P : (a + 1) * P].rearrange("(o one) -> o one", one=1)
+            )
+            out_bias_bf.append(bias_bf)
+
+        w_planes = consts.tile([P, IN_PASSES, HID], U8, align_bytes=64)
+        nc.vector.memset(w_planes[:].bitcast(I32), 0)
+
+        x_raws = [load_x(0)]
+
+        w_words = consts.tile([P, IN_PASSES, HID], U32, align_bytes=64)
+        for g in range(IN_PASSES):
+            nc.sync.dma_start(
+                out=w_words[:, g, :].bitcast(I32),
+                in_=w_in_words[g].rearrange("p n t -> p (n t)").bitcast(I32),
+            )
+        for quadrant in range(4):
+            nc.sync.dma_start(
+                out=w_planes[32 * quadrant : 32 * quadrant + 4, :, :].bitcast(I32),
+                in_=w_in_scales[:, 4 * quadrant : 4 * quadrant + 4, :].rearrange("g r n -> r g n").bitcast(I32),
+            )
+
+        ow_raw = consts.tile([P, O_TILES, HID * K], BF16)
+        nc.sync.dma_start(out=ow_raw[:], in_=out_weight.rearrange("(a o) c k -> o a (c k)", o=P))
+
+        for chunk in range(1, B * CHUNKS_PER_IMAGE):
+            x_raws.append(load_x(chunk))
+
+        lw = consts.tile([P, K], F32)
+        nc.vector.tensor_copy(out=lw[:], in_=lw_bf[:])
+        neg_lw = consts.tile([P, K], F32)
+        nc.vector.tensor_scalar(out=neg_lw[:], in0=lw[:], scalar1=-1.0, scalar2=None, op0=ALU.mult)
+        neg_abs = consts.tile([P, K], F32)
+        nc.vector.tensor_tensor(out=neg_abs[:], in0=lw[:], in1=neg_lw[:], op=ALU.min)
+        tail = consts.tile([P, K], F32)
+        nc.scalar.activation(out=tail[:], in_=neg_abs[:], func=ACT.Exp)
+        nc.vector.tensor_scalar(out=tail[:], in0=tail[:], scalar1=1.0, scalar2=None, op0=ALU.add)
+        nc.scalar.activation(out=tail[:], in_=tail[:], func=ACT.Ln)
+        widths = consts.tile([P, K], F32)
+        nc.vector.tensor_scalar(out=widths[:], in0=lw[:], scalar1=0.0, scalar2=None, op0=ALU.max)
+        nc.vector.tensor_tensor(out=widths[:], in0=widths[:], in1=tail[:], op=ALU.add)
+        nc.vector.tensor_scalar(out=widths[:], in0=widths[:], scalar1=1e-4, scalar2=None, op0=ALU.add)
+        inv_w = consts.tile([P, K], F32)
+        nc.vector.reciprocal(out=inv_w[:], in_=widths[:])
+        b_in_f = consts.tile([P, 1], F32)
+        nc.vector.tensor_copy(out=b_in_f[:], in_=b_in_bf[:])
+        shift = consts.tile([P, K], F32)
+        nc.vector.tensor_scalar(
+            out=shift[:], in0=centers_bf[:], scalar1=-1.0, scalar2=b_in_f[:, 0:1], op0=ALU.mult, op1=ALU.add
+        )
+        shift_w = consts.tile([P, K], F32)
+        nc.vector.tensor_tensor(out=shift_w[:], in0=shift[:], in1=inv_w[:], op=ALU.mult)
+        out_bias_f = []
+        for a in range(O_TILES):
+            bias_f = consts.tile([P, 1], F32, name="out_bias_f%d" % a)
+            nc.vector.tensor_copy(out=bias_f[:], in_=out_bias_bf[a][:])
+            out_bias_f.append(bias_f)
+
+        ident = consts.tile([P, P], F32)
+        make_identity(nc, ident[:])
+        ow_grouped = consts.tile([P, O_TILES, RBF_PASSES, P, 2], F32, align_bytes=64)
+        for a in range(O_TILES):
+            ow_pairs = ow_raw[:, a, :].bitcast(F32)
+            ow_t = out_banks.tile([P, RBF_PASSES, 2, P], F32, name="ow_t", tag="out_ps")
+            for h in range(RBF_PASSES):
+                for u in range(2):
+                    nc.tensor.transpose(ow_t[:, h, u, :], ow_pairs[:, 2 * h + u : HID * K // 2 : 4], ident[:])
+            nc.scalar.copy(out=ow_grouped[:, a], in_=ow_t[:].rearrange("c h u o -> c h o u"))
+        ow_codes = consts.tile([P, O_TILES, RBF_PASSES, P], U32, align_bytes=64)
+        ow_scales = consts.tile([P, O_TILES, RBF_PASSES, P], U8, align_bytes=64)
+        nc.vector.quantize_mx(
+            out=ow_codes[:].rearrange("c a h o -> c (a h o)").bitcast(FP8X4),
+            scales=ow_scales[:].rearrange("c a h o -> c (a h o)"),
+            in_=ow_grouped[:].rearrange("c a h o u -> c (a h o u)").bitcast(BF16),
+        )
+
+        for chunk in range(B * CHUNKS_PER_IMAGE):
+            x_raw = x_raws[chunk]
+            x_grouped = work.tile([P, IN_PASSES, PIX, PACK], BF16, align_bytes=64)
+            for g in range(IN_PASSES):
+                nc.vector.tensor_copy(
+                    out=x_grouped[:, g].rearrange("p (n i) t -> p n t i", i=RUN),
+                    in_=x_raw[:, g].rearrange("p t (n i) -> p n t i", i=RUN),
+                )
+            x_codes = work.tile([P, IN_PASSES, PIX], U32, align_bytes=64)
+            x_scales = work.tile([P, IN_PASSES, PIX], U8, align_bytes=64)
+            nc.vector.quantize_mx(
+                out=x_codes[:].rearrange("p g n -> p (g n)").bitcast(FP8X4),
+                scales=x_scales[:].rearrange("p g n -> p (g n)"),
+                in_=x_grouped[:].rearrange("p g n t -> p (g n t)"),
+            )
+
+            z_scalar = z_banks.tile([P, PIX], F32)
+            z_vector = z_banks.tile([P, PIX], F32)
+            for z_bank in (z_scalar, z_vector):
+                for g in range(IN_PASSES):
+                    nc.tensor.matmul_mx(
+                        out=z_bank[:],
+                        lhsT=w_words[:, g, :].bitcast(FP8X4),
+                        lhsT_scale=w_planes[:, g, :],
+                        rhs=x_codes[:, g, :].bitcast(FP8X4),
+                        rhs_scale=x_scales[:, g, :],
+                        start=(g == 0),
+                        stop=(g == IN_PASSES - 1),
+                    )
+
+            squares = work.tile([P, K, PIX], F32)
+            for k in range(K_ON_SCALAR):
+                nc.scalar.activation(
+                    out=squares[:, k, :],
+                    in_=z_scalar[:],
+                    func=ACT.Square,
+                    scale=inv_w[:, k : k + 1],
+                    bias=shift_w[:, k : k + 1],
+                )
+            for k in range(K_ON_SCALAR, K):
+                scaled = work.tile([P, PIX], F32)
+                nc.vector.tensor_scalar(
+                    out=scaled[:],
+                    in0=z_vector[:],
+                    scalar1=shift[:, k : k + 1],
+                    scalar2=inv_w[:, k : k + 1],
+                    op0=ALU.add,
+                    op1=ALU.mult,
+                )
+                nc.vector.tensor_tensor(out=squares[:, k, :], in0=scaled[:], in1=scaled[:], op=ALU.mult)
+
+            phi_grouped = work.tile([P, RBF_PASSES, PIX, PACK], BF16, align_bytes=64)
+            phi_codes = work.tile([P, RBF_PASSES, PIX], U32, align_bytes=64)
+            phi_scales = work.tile([P, RBF_PASSES, PIX], U8, align_bytes=64)
+            for h in range(RBF_PASSES):
+                nc.scalar.activation(
+                    out=phi_grouped[:, h].rearrange("c (n i) t -> c n t i", i=RUN),
+                    in_=squares[:, PACK * h : PACK * (h + 1), :].rearrange("c t (n i) -> c n t i", i=RUN),
+                    func=ACT.Exp,
+                    scale=-1.0,
+                )
+                nc.vector.quantize_mx(
+                    out=phi_codes[:, h, :].bitcast(FP8X4),
+                    scales=phi_scales[:, h, :],
+                    in_=phi_grouped[:, h].rearrange("c n t -> c (n t)"),
+                )
+
+            image_out = out[chunk // CHUNKS_PER_IMAGE].rearrange("(a o) h w -> a o (h w)", o=P)
+            first = (chunk % CHUNKS_PER_IMAGE) * PIX
+            for a in range(O_TILES):
+                out_ps = out_banks.tile([P, PIX], F32)
+                for h in range(RBF_PASSES):
+                    nc.tensor.matmul_mx(
+                        out=out_ps[:],
+                        lhsT=ow_codes[:, a, h, :].bitcast(FP8X4),
+                        lhsT_scale=ow_scales[:, a, h, :],
+                        rhs=phi_codes[:, h, :].bitcast(FP8X4),
+                        rhs_scale=phi_scales[:, h, :],
+                        start=(h == 0),
+                        stop=(h == RBF_PASSES - 1),
+                    )
+                out_sb = stores.tile([P, PIX], F32)
+                nc.vector.tensor_scalar(
+                    out=out_sb[:], in0=out_ps[:], scalar1=out_bias_f[a][:, 0:1], scalar2=None, op0=ALU.add
+                )
+                nc.sync.dma_start(out=image_out[a, :, first : first + PIX], in_=out_sb[:])

@@ -19,32 +19,38 @@ K_PASS = P * PACK
 IN_PASSES = C_IN // K_PASS
 RBF_PASSES = HID * K // K_PASS
 O_TILES = C_OUT // P
-PIX = 512
-CHUNKS_PER_IMAGE = HW // PIX
+BANK = 512
 RUN = 4
 K_ON_SCALAR = 6
 
 FLOPS = 2 * B * HW * C_IN * HID + 2 * B * HW * HID * K * C_OUT
 
 
+def pixel_chunks():
+    return [(image, first, BANK) for image in range(B) for first in range(0, HW, BANK)]
+
+
 def tile_rbfkanhead_kernel(
     tc, x, w_in_words, w_in_scales, b_in, centers, log_widths, out_weight, out_bias, out
 ):
     nc = tc.nc
+    chunks = pixel_chunks()
+    n_chunks = len(chunks)
     with ExitStack() as ctx:
+        ctx.enter_context(tc.manual_schedule())
         consts = ctx.enter_context(tc.tile_pool(name="consts", bufs=1))
-        x_pool = ctx.enter_context(tc.tile_pool(name="x_pool", bufs=B * CHUNKS_PER_IMAGE))
+        x_pool = ctx.enter_context(tc.tile_pool(name="x_pool", bufs=n_chunks))
         work = ctx.enter_context(tc.tile_pool(name="work", bufs=2))
         stores = ctx.enter_context(tc.tile_pool(name="stores", bufs=4))
         z_banks = ctx.enter_context(tc.psum_pool(name="z_banks", bufs=2))
         out_banks = ctx.enter_context(tc.psum_pool(name="out_banks", bufs=4))
 
         def load_x(chunk):
-            image = x[chunk // CHUNKS_PER_IMAGE].rearrange("(g p t) h w -> g p t (h w)", p=P, t=PACK)
-            first = (chunk % CHUNKS_PER_IMAGE) * PIX
-            x_raw = x_pool.tile([P, IN_PASSES, PACK, PIX], BF16, name="x_raw")
+            image, first, width = chunks[chunk]
+            rows = x[image].rearrange("(g p t) h w -> g p t (h w)", p=P, t=PACK)
+            x_raw = x_pool.tile([P, IN_PASSES, PACK, width], BF16, name="x_raw")
             for g in range(IN_PASSES):
-                nc.sync.dma_start(out=x_raw[:, g], in_=image[g, :, :, first : first + PIX])
+                nc.sync.dma_start(out=x_raw[:, g], in_=rows[g, :, :, first : first + width])
             return x_raw
 
         lw_bf = consts.tile([P, K], BF16)
@@ -63,9 +69,10 @@ def tile_rbfkanhead_kernel(
 
         w_planes = consts.tile([P, IN_PASSES, HID], U8, align_bytes=64)
         nc.vector.memset(w_planes[:].bitcast(I32), 0)
+        ones = consts.tile([P, 1], F32)
+        nc.vector.memset(ones[:], 1.0)
 
         x_raws = [load_x(0)]
-
         w_words = consts.tile([P, IN_PASSES, HID], U32, align_bytes=64)
         for g in range(IN_PASSES):
             nc.sync.dma_start(
@@ -77,45 +84,161 @@ def tile_rbfkanhead_kernel(
                 out=w_planes[32 * quadrant : 32 * quadrant + 4, :, :].bitcast(I32),
                 in_=w_in_scales[:, 4 * quadrant : 4 * quadrant + 4, :].rearrange("g r n -> r g n").bitcast(I32),
             )
-
         ow_raw = consts.tile([P, O_TILES, HID * K], BF16)
         nc.sync.dma_start(out=ow_raw[:], in_=out_weight.rearrange("(a o) c k -> o a (c k)", o=P))
-
-        for chunk in range(1, B * CHUNKS_PER_IMAGE):
+        for chunk in range(1, n_chunks):
             x_raws.append(load_x(chunk))
 
-        lw = consts.tile([P, K], F32)
-        nc.vector.tensor_copy(out=lw[:], in_=lw_bf[:])
-        neg_lw = consts.tile([P, K], F32)
-        nc.vector.tensor_scalar(out=neg_lw[:], in0=lw[:], scalar1=-1.0, scalar2=None, op0=ALU.mult)
-        neg_abs = consts.tile([P, K], F32)
-        nc.vector.tensor_tensor(out=neg_abs[:], in0=lw[:], in1=neg_lw[:], op=ALU.min)
+        ident = consts.tile([P, P], F32)
+        make_identity(nc, ident[:])
+
         tail = consts.tile([P, K], F32)
-        nc.scalar.activation(out=tail[:], in_=neg_abs[:], func=ACT.Exp)
-        nc.vector.tensor_scalar(out=tail[:], in0=tail[:], scalar1=1.0, scalar2=None, op0=ALU.add)
-        nc.scalar.activation(out=tail[:], in_=tail[:], func=ACT.Ln)
+        nc.scalar.activation(out=tail[:], in_=lw_bf[:], func=ACT.Abs)
+        nc.scalar.activation(out=tail[:], in_=tail[:], func=ACT.Exp, scale=-1.0)
+        nc.scalar.activation(out=tail[:], in_=tail[:], func=ACT.Ln, bias=ones[:, 0:1])
+        table_warmer = consts.tile([P, 1], F32)
+        nc.scalar.activation(out=table_warmer[:], in_=ones[:], func=ACT.Exp)
         widths = consts.tile([P, K], F32)
-        nc.vector.tensor_scalar(out=widths[:], in0=lw[:], scalar1=0.0, scalar2=None, op0=ALU.max)
-        nc.vector.tensor_tensor(out=widths[:], in0=widths[:], in1=tail[:], op=ALU.add)
-        nc.vector.tensor_scalar(out=widths[:], in0=widths[:], scalar1=1e-4, scalar2=None, op0=ALU.add)
-        inv_w = consts.tile([P, K], F32)
-        nc.vector.reciprocal(out=inv_w[:], in_=widths[:])
+        nc.vector.tensor_scalar(out=widths[:], in0=lw_bf[:], scalar1=0.0, scalar2=None, op0=ALU.max)
         b_in_f = consts.tile([P, 1], F32)
         nc.vector.tensor_copy(out=b_in_f[:], in_=b_in_bf[:])
         shift = consts.tile([P, K], F32)
         nc.vector.tensor_scalar(
             out=shift[:], in0=centers_bf[:], scalar1=-1.0, scalar2=b_in_f[:, 0:1], op0=ALU.mult, op1=ALU.add
         )
-        shift_w = consts.tile([P, K], F32)
-        nc.vector.tensor_tensor(out=shift_w[:], in0=shift[:], in1=inv_w[:], op=ALU.mult)
         out_bias_f = []
         for a in range(O_TILES):
             bias_f = consts.tile([P, 1], F32, name="out_bias_f%d" % a)
             nc.vector.tensor_copy(out=bias_f[:], in_=out_bias_bf[a][:])
             out_bias_f.append(bias_f)
+        nc.vector.tensor_tensor(out=widths[:], in0=widths[:], in1=tail[:], op=ALU.add)
+        nc.vector.tensor_scalar(out=widths[:], in0=widths[:], scalar1=1e-4, scalar2=None, op0=ALU.add)
+        inv_w = consts.tile([P, K], F32)
+        nc.vector.reciprocal(out=inv_w[:], in_=widths[:])
+        shift_w = consts.tile([P, K], F32)
+        nc.vector.tensor_tensor(out=shift_w[:], in0=shift[:], in1=inv_w[:], op=ALU.mult)
 
-        ident = consts.tile([P, P], F32)
-        make_identity(nc, ident[:])
+        x_grouped, x_codes, x_scales = {}, {}, {}
+        z_scalar, z_vector = {}, {}
+        squares, phi_grouped, phi_codes, phi_scales, out_ps = {}, {}, {}, {}, {}
+
+        def regroup_x(chunk):
+            width = chunks[chunk][2]
+            x_grouped[chunk] = work.tile([P, IN_PASSES, width, PACK], BF16, align_bytes=64, name="x_grouped")
+            x_codes[chunk] = work.tile([P, IN_PASSES, width], U32, align_bytes=64, name="x_codes")
+            x_scales[chunk] = work.tile([P, IN_PASSES, width], U8, align_bytes=64, name="x_scales")
+            for g in range(IN_PASSES):
+                nc.vector.tensor_copy(
+                    out=x_grouped[chunk][:, g].rearrange("p (n i) t -> p n t i", i=RUN),
+                    in_=x_raws[chunk][:, g].rearrange("p t (n i) -> p n t i", i=RUN),
+                )
+
+        def quantise_x(chunk, g):
+            nc.vector.quantize_mx(
+                out=x_codes[chunk][:, g, :].bitcast(FP8X4),
+                scales=x_scales[chunk][:, g, :],
+                in_=x_grouped[chunk][:, g].rearrange("p n t -> p (n t)"),
+            )
+
+        def first_contraction(chunk):
+            width = chunks[chunk][2]
+            z_scalar[chunk] = z_banks.tile([P, width], F32, name="z_scalar")
+            z_vector[chunk] = z_banks.tile([P, width], F32, name="z_vector")
+            for z_bank in (z_scalar[chunk], z_vector[chunk]):
+                for g in range(IN_PASSES):
+                    nc.tensor.matmul_mx(
+                        out=z_bank[:],
+                        lhsT=w_words[:, g, :].bitcast(FP8X4),
+                        lhsT_scale=w_planes[:, g, :],
+                        rhs=x_codes[chunk][:, g, :].bitcast(FP8X4),
+                        rhs_scale=x_scales[chunk][:, g, :],
+                        start=(g == 0),
+                        stop=(g == IN_PASSES - 1),
+                    )
+
+        def squares_on_scalar(chunk):
+            squares[chunk] = work.tile([P, K, chunks[chunk][2]], F32, name="squares")
+            for k in range(K_ON_SCALAR):
+                nc.scalar.activation(
+                    out=squares[chunk][:, k, :],
+                    in_=z_scalar[chunk][:],
+                    func=ACT.Square,
+                    scale=inv_w[:, k : k + 1],
+                    bias=shift_w[:, k : k + 1],
+                )
+
+        def squares_on_vector(chunk):
+            scaled = work.tile([P, K - K_ON_SCALAR, chunks[chunk][2]], F32, name="scaled")
+            for k in range(K_ON_SCALAR, K):
+                nc.vector.tensor_scalar(
+                    out=scaled[:, k - K_ON_SCALAR, :],
+                    in0=z_vector[chunk][:],
+                    scalar1=shift[:, k : k + 1],
+                    scalar2=inv_w[:, k : k + 1],
+                    op0=ALU.add,
+                    op1=ALU.mult,
+                )
+            for k in range(K_ON_SCALAR, K):
+                nc.vector.tensor_tensor(
+                    out=squares[chunk][:, k, :],
+                    in0=scaled[:, k - K_ON_SCALAR, :],
+                    in1=scaled[:, k - K_ON_SCALAR, :],
+                    op=ALU.mult,
+                )
+
+        def exponentials(chunk, h):
+            width = chunks[chunk][2]
+            if h == 0:
+                phi_grouped[chunk] = work.tile([P, RBF_PASSES, width, PACK], BF16, align_bytes=64, name="phi_grouped")
+                phi_codes[chunk] = work.tile([P, RBF_PASSES, width], U32, align_bytes=64, name="phi_codes")
+                phi_scales[chunk] = work.tile([P, RBF_PASSES, width], U8, align_bytes=64, name="phi_scales")
+            nc.scalar.activation(
+                out=phi_grouped[chunk][:, h].rearrange("c (n i) t -> c n t i", i=RUN),
+                in_=squares[chunk][:, PACK * h : PACK * (h + 1), :].rearrange("c t (n i) -> c n t i", i=RUN),
+                func=ACT.Exp,
+                scale=-1.0,
+            )
+
+        def second_contraction(chunk, h):
+            nc.vector.quantize_mx(
+                out=phi_codes[chunk][:, h, :].bitcast(FP8X4),
+                scales=phi_scales[chunk][:, h, :],
+                in_=phi_grouped[chunk][:, h].rearrange("c n t -> c (n t)"),
+            )
+            if h == 0:
+                out_ps[chunk] = [
+                    out_banks.tile([P, chunks[chunk][2]], F32, name="out_ps") for a in range(O_TILES)
+                ]
+            for a in range(O_TILES):
+                nc.tensor.matmul_mx(
+                    out=out_ps[chunk][a][:],
+                    lhsT=ow_codes[:, a, h, :].bitcast(FP8X4),
+                    lhsT_scale=ow_scales[:, a, h, :],
+                    rhs=phi_codes[chunk][:, h, :].bitcast(FP8X4),
+                    rhs_scale=phi_scales[chunk][:, h, :],
+                    start=(h == 0),
+                    stop=(h == RBF_PASSES - 1),
+                )
+
+        def bias_and_store(chunk, a, on_scalar=False):
+            image, first, width = chunks[chunk]
+            out_sb = stores.tile([P, width], F32, name="out_sb")
+            if on_scalar:
+                nc.scalar.activation(
+                    out=out_sb[:], in_=out_ps[chunk][a][:], func=ACT.Identity, bias=out_bias_f[a][:, 0:1]
+                )
+            else:
+                nc.vector.tensor_scalar(
+                    out=out_sb[:], in0=out_ps[chunk][a][:], scalar1=out_bias_f[a][:, 0:1], scalar2=None, op0=ALU.add
+                )
+            rows = out[image].rearrange("(a o) h w -> a o (h w)", o=P)
+            nc.sync.dma_start(out=rows[a, :, first : first + width], in_=out_sb[:])
+
+        regroup_x(0)
+        for g in range(IN_PASSES):
+            quantise_x(0, g)
+        first_contraction(0)
+
         ow_grouped = consts.tile([P, O_TILES, RBF_PASSES, P, 2], F32, align_bytes=64)
         for a in range(O_TILES):
             ow_pairs = ow_raw[:, a, :].bitcast(F32)
@@ -123,7 +246,7 @@ def tile_rbfkanhead_kernel(
             for h in range(RBF_PASSES):
                 for u in range(2):
                     nc.tensor.transpose(ow_t[:, h, u, :], ow_pairs[:, 2 * h + u : HID * K // 2 : 4], ident[:])
-            nc.scalar.copy(out=ow_grouped[:, a], in_=ow_t[:].rearrange("c h u o -> c h o u"))
+            nc.vector.tensor_copy(out=ow_grouped[:, a], in_=ow_t[:].rearrange("c h u o -> c h o u"))
         ow_codes = consts.tile([P, O_TILES, RBF_PASSES, P], U32, align_bytes=64)
         ow_scales = consts.tile([P, O_TILES, RBF_PASSES, P], U8, align_bytes=64)
         nc.vector.quantize_mx(
@@ -132,89 +255,24 @@ def tile_rbfkanhead_kernel(
             in_=ow_grouped[:].rearrange("c a h o u -> c (a h o u)").bitcast(BF16),
         )
 
-        for chunk in range(B * CHUNKS_PER_IMAGE):
-            x_raw = x_raws[chunk]
-            x_grouped = work.tile([P, IN_PASSES, PIX, PACK], BF16, align_bytes=64)
-            for g in range(IN_PASSES):
-                nc.vector.tensor_copy(
-                    out=x_grouped[:, g].rearrange("p (n i) t -> p n t i", i=RUN),
-                    in_=x_raw[:, g].rearrange("p t (n i) -> p n t i", i=RUN),
-                )
-            x_codes = work.tile([P, IN_PASSES, PIX], U32, align_bytes=64)
-            x_scales = work.tile([P, IN_PASSES, PIX], U8, align_bytes=64)
-            nc.vector.quantize_mx(
-                out=x_codes[:].rearrange("p g n -> p (g n)").bitcast(FP8X4),
-                scales=x_scales[:].rearrange("p g n -> p (g n)"),
-                in_=x_grouped[:].rearrange("p g n t -> p (g n t)"),
-            )
-
-            z_scalar = z_banks.tile([P, PIX], F32)
-            z_vector = z_banks.tile([P, PIX], F32)
-            for z_bank in (z_scalar, z_vector):
-                for g in range(IN_PASSES):
-                    nc.tensor.matmul_mx(
-                        out=z_bank[:],
-                        lhsT=w_words[:, g, :].bitcast(FP8X4),
-                        lhsT_scale=w_planes[:, g, :],
-                        rhs=x_codes[:, g, :].bitcast(FP8X4),
-                        rhs_scale=x_scales[:, g, :],
-                        start=(g == 0),
-                        stop=(g == IN_PASSES - 1),
-                    )
-
-            squares = work.tile([P, K, PIX], F32)
-            for k in range(K_ON_SCALAR):
-                nc.scalar.activation(
-                    out=squares[:, k, :],
-                    in_=z_scalar[:],
-                    func=ACT.Square,
-                    scale=inv_w[:, k : k + 1],
-                    bias=shift_w[:, k : k + 1],
-                )
-            for k in range(K_ON_SCALAR, K):
-                scaled = work.tile([P, PIX], F32)
-                nc.vector.tensor_scalar(
-                    out=scaled[:],
-                    in0=z_vector[:],
-                    scalar1=shift[:, k : k + 1],
-                    scalar2=inv_w[:, k : k + 1],
-                    op0=ALU.add,
-                    op1=ALU.mult,
-                )
-                nc.vector.tensor_tensor(out=squares[:, k, :], in0=scaled[:], in1=scaled[:], op=ALU.mult)
-
-            phi_grouped = work.tile([P, RBF_PASSES, PIX, PACK], BF16, align_bytes=64)
-            phi_codes = work.tile([P, RBF_PASSES, PIX], U32, align_bytes=64)
-            phi_scales = work.tile([P, RBF_PASSES, PIX], U8, align_bytes=64)
+        for chunk in range(n_chunks):
+            squares_on_scalar(chunk)
+            if chunk > 0:
+                second_contraction(chunk - 1, RBF_PASSES - 1)
+            squares_on_vector(chunk)
+            if chunk + 1 < n_chunks:
+                regroup_x(chunk + 1)
+            for step in range(IN_PASSES):
+                if chunk + 1 < n_chunks:
+                    quantise_x(chunk + 1, step)
+                if chunk > 0:
+                    bias_and_store(chunk - 1, step)
+            if chunk + 1 < n_chunks:
+                first_contraction(chunk + 1)
             for h in range(RBF_PASSES):
-                nc.scalar.activation(
-                    out=phi_grouped[:, h].rearrange("c (n i) t -> c n t i", i=RUN),
-                    in_=squares[:, PACK * h : PACK * (h + 1), :].rearrange("c t (n i) -> c n t i", i=RUN),
-                    func=ACT.Exp,
-                    scale=-1.0,
-                )
-                nc.vector.quantize_mx(
-                    out=phi_codes[:, h, :].bitcast(FP8X4),
-                    scales=phi_scales[:, h, :],
-                    in_=phi_grouped[:, h].rearrange("c n t -> c (n t)"),
-                )
-
-            image_out = out[chunk // CHUNKS_PER_IMAGE].rearrange("(a o) h w -> a o (h w)", o=P)
-            first = (chunk % CHUNKS_PER_IMAGE) * PIX
-            for a in range(O_TILES):
-                out_ps = out_banks.tile([P, PIX], F32)
-                for h in range(RBF_PASSES):
-                    nc.tensor.matmul_mx(
-                        out=out_ps[:],
-                        lhsT=ow_codes[:, a, h, :].bitcast(FP8X4),
-                        lhsT_scale=ow_scales[:, a, h, :],
-                        rhs=phi_codes[:, h, :].bitcast(FP8X4),
-                        rhs_scale=phi_scales[:, h, :],
-                        start=(h == 0),
-                        stop=(h == RBF_PASSES - 1),
-                    )
-                out_sb = stores.tile([P, PIX], F32)
-                nc.vector.tensor_scalar(
-                    out=out_sb[:], in0=out_ps[:], scalar1=out_bias_f[a][:, 0:1], scalar2=None, op0=ALU.add
-                )
-                nc.sync.dma_start(out=image_out[a, :, first : first + PIX], in_=out_sb[:])
+                exponentials(chunk, h)
+                if h < RBF_PASSES - 1:
+                    second_contraction(chunk, h)
+        second_contraction(n_chunks - 1, RBF_PASSES - 1)
+        bias_and_store(n_chunks - 1, 0)
+        bias_and_store(n_chunks - 1, 1, on_scalar=True)

@@ -21,7 +21,7 @@ RBF_PASSES = HID * K // K_PASS
 O_TILES = C_OUT // P
 BANK = 512
 RUN = 4
-K_ON_SCALAR = 6
+K_ON_SCALAR = 5
 
 FLOPS = 2 * B * HW * C_IN * HID + 2 * B * HW * HID * K * C_OUT
 

@@ -21,7 +21,7 @@ RBF_PASSES = HID * K // K_PASS
 O_TILES = C_OUT // P
 BANK = 512
 RUN = 4
-K_ON_SCALAR = 5
+K_ON_SCALAR = 6
 
 FLOPS = 2 * B * HW * C_IN * HID + 2 * B * HW * HID * K * C_OUT
 
@@ -157,11 +157,11 @@ def tile_rbfkanhead_kernel(
                     )
 
         def squares_on_scalar(chunk):
-            squares[chunk] = work.tile([P, K, chunks[chunk][2]], F32, name="squares")
+            squares[chunk] = work.tile([P, RBF_PASSES, chunks[chunk][2] // RUN, PACK, RUN], F32, name="squares")
             for k in range(K_ON_SCALAR):
                 nc.scalar.activation(
-                    out=squares[chunk][:, k, :],
-                    in_=z_scalar[chunk][:],
+                    out=squares[chunk][:, k // PACK, :, k % PACK, :],
+                    in_=z_scalar[chunk][:].rearrange("c (n i) -> c n i", i=RUN),
                     func=ACT.Square,
                     scale=inv_w[:, k : k + 1],
                     bias=shift_w[:, k : k + 1],
@@ -180,9 +180,9 @@ def tile_rbfkanhead_kernel(
                 )
             for k in range(K_ON_SCALAR, K):
                 nc.vector.tensor_tensor(
-                    out=squares[chunk][:, k, :],
-                    in0=scaled[:, k - K_ON_SCALAR, :],
-                    in1=scaled[:, k - K_ON_SCALAR, :],
+                    out=squares[chunk][:, k // PACK, :, k % PACK, :],
+                    in0=scaled[:, k - K_ON_SCALAR, :].rearrange("c (n i) -> c n i", i=RUN),
+                    in1=scaled[:, k - K_ON_SCALAR, :].rearrange("c (n i) -> c n i", i=RUN),
                     op=ALU.mult,
                 )
 
@@ -194,7 +194,7 @@ def tile_rbfkanhead_kernel(
                 phi_scales[chunk] = work.tile([P, RBF_PASSES, width], U8, align_bytes=64, name="phi_scales")
             nc.scalar.activation(
                 out=phi_grouped[chunk][:, h].rearrange("c (n i) t -> c n t i", i=RUN),
-                in_=squares[chunk][:, PACK * h : PACK * (h + 1), :].rearrange("c t (n i) -> c n t i", i=RUN),
+                in_=squares[chunk][:, h],
                 func=ACT.Exp,
                 scale=-1.0,
             )

@@ -19,36 +19,35 @@ K_PASS = P * PACK
 IN_PASSES = C_IN // K_PASS
 RBF_PASSES = HID * K // K_PASS
 O_TILES = C_OUT // P
-BANK = 512
 RUN = 4
-K_ON_SCALAR = 6
+
+CHUNKS = (
+    (0, 0, 512, 2),
+    (0, 512, 512, 2),
+    (1, 0, 512, 2),
+    (1, 512, 512, 2),
+)
 
 FLOPS = 2 * B * HW * C_IN * HID + 2 * B * HW * HID * K * C_OUT
-
-
-def pixel_chunks():
-    return [(image, first, BANK) for image in range(B) for first in range(0, HW, BANK)]
 
 
 def tile_rbfkanhead_kernel(
     tc, x, w_in_words, w_in_scales, b_in, centers, log_widths, out_weight, out_bias, out
 ):
     nc = tc.nc
-    chunks = pixel_chunks()
-    n_chunks = len(chunks)
+    n_chunks = len(CHUNKS)
     with ExitStack() as ctx:
         ctx.enter_context(tc.manual_schedule())
         consts = ctx.enter_context(tc.tile_pool(name="consts", bufs=1))
-        x_pool = ctx.enter_context(tc.tile_pool(name="x_pool", bufs=n_chunks))
         work = ctx.enter_context(tc.tile_pool(name="work", bufs=2))
         stores = ctx.enter_context(tc.tile_pool(name="stores", bufs=4))
         z_banks = ctx.enter_context(tc.psum_pool(name="z_banks", bufs=2))
         out_banks = ctx.enter_context(tc.psum_pool(name="out_banks", bufs=4))
 
         def load_x(chunk):
-            image, first, width = chunks[chunk]
+            image, first, width, on_vector = CHUNKS[chunk]
             rows = x[image].rearrange("(g p t) h w -> g p t (h w)", p=P, t=PACK)
-            x_raw = x_pool.tile([P, IN_PASSES, PACK, width], BF16, name="x_raw")
+            x_raw = consts.tile([P, IN_PASSES, PACK, width], BF16, name="x_raw%d" % chunk)
             for g in range(IN_PASSES):
                 nc.sync.dma_start(out=x_raw[:, g], in_=rows[g, :, :, first : first + width])
             return x_raw
@@ -84,67 +83,46 @@ def tile_rbfkanhead_kernel(
                 out=w_planes[32 * quadrant : 32 * quadrant + 4, :, :].bitcast(I32),
                 in_=w_in_scales[:, 4 * quadrant : 4 * quadrant + 4, :].rearrange("g r n -> r g n").bitcast(I32),
             )
+        x_raws.append(load_x(1))
         ow_raw = consts.tile([P, O_TILES, HID * K], BF16)
         nc.sync.dma_start(out=ow_raw[:], in_=out_weight.rearrange("(a o) c k -> o a (c k)", o=P))
-        for chunk in range(1, n_chunks):
+        for chunk in range(2, n_chunks):
             x_raws.append(load_x(chunk))
 
         ident = consts.tile([P, P], F32)
         make_identity(nc, ident[:])
 
-        tail = consts.tile([P, K], F32)
-        nc.scalar.activation(out=tail[:], in_=lw_bf[:], func=ACT.Abs)
-        nc.scalar.activation(out=tail[:], in_=tail[:], func=ACT.Exp, scale=-1.0)
-        nc.scalar.activation(out=tail[:], in_=tail[:], func=ACT.Ln, bias=ones[:, 0:1])
-        table_warmer = consts.tile([P, 1], F32)
-        nc.scalar.activation(out=table_warmer[:], in_=ones[:], func=ACT.Exp)
-        widths = consts.tile([P, K], F32)
-        nc.vector.tensor_scalar(out=widths[:], in0=lw_bf[:], scalar1=0.0, scalar2=None, op0=ALU.max)
-        b_in_f = consts.tile([P, 1], F32)
-        nc.vector.tensor_copy(out=b_in_f[:], in_=b_in_bf[:])
-        shift = consts.tile([P, K], F32)
-        nc.vector.tensor_scalar(
-            out=shift[:], in0=centers_bf[:], scalar1=-1.0, scalar2=b_in_f[:, 0:1], op0=ALU.mult, op1=ALU.add
-        )
-        out_bias_f = []
-        for a in range(O_TILES):
-            bias_f = consts.tile([P, 1], F32, name="out_bias_f%d" % a)
-            nc.vector.tensor_copy(out=bias_f[:], in_=out_bias_bf[a][:])
-            out_bias_f.append(bias_f)
-        nc.vector.tensor_tensor(out=widths[:], in0=widths[:], in1=tail[:], op=ALU.add)
-        nc.vector.tensor_scalar(out=widths[:], in0=widths[:], scalar1=1e-4, scalar2=None, op0=ALU.add)
-        inv_w = consts.tile([P, K], F32)
-        nc.vector.reciprocal(out=inv_w[:], in_=widths[:])
-        shift_w = consts.tile([P, K], F32)
-        nc.vector.tensor_tensor(out=shift_w[:], in0=shift[:], in1=inv_w[:], op=ALU.mult)
-
         x_grouped, x_codes, x_scales = {}, {}, {}
         z_scalar, z_vector = {}, {}
-        squares, phi_grouped, phi_codes, phi_scales, out_ps = {}, {}, {}, {}, {}
+        squares, scaled, phi_grouped, phi_codes, phi_scales, out_ps = {}, {}, {}, {}, {}, {}
 
-        def regroup_x(chunk):
-            width = chunks[chunk][2]
-            x_grouped[chunk] = work.tile([P, IN_PASSES, width, PACK], BF16, align_bytes=64, name="x_grouped")
-            x_codes[chunk] = work.tile([P, IN_PASSES, width], U32, align_bytes=64, name="x_codes")
-            x_scales[chunk] = work.tile([P, IN_PASSES, width], U8, align_bytes=64, name="x_scales")
-            for g in range(IN_PASSES):
-                nc.vector.tensor_copy(
-                    out=x_grouped[chunk][:, g].rearrange("p (n i) t -> p n t i", i=RUN),
-                    in_=x_raws[chunk][:, g].rearrange("p t (n i) -> p n t i", i=RUN),
-                )
+        def regroup_x(chunk, g):
+            width = CHUNKS[chunk][2]
+            if g == 0:
+                x_grouped[chunk] = work.tile([P, IN_PASSES, width, PACK], BF16, align_bytes=64, name="x_grouped")
+            nc.vector.tensor_copy(
+                out=x_grouped[chunk][:, g].rearrange("p (n i) t -> p n t i", i=RUN),
+                in_=x_raws[chunk][:, g].rearrange("p t (n i) -> p n t i", i=RUN),
+            )
 
-        def quantise_x(chunk, g):
+        def quantise_x(chunk):
+            width = CHUNKS[chunk][2]
+            x_codes[chunk] = consts.tile([P, IN_PASSES, width], U32, align_bytes=64, name="x_codes%d" % chunk)
+            x_scales[chunk] = consts.tile([P, IN_PASSES, width], U8, align_bytes=64, name="x_scales%d" % chunk)
             nc.vector.quantize_mx(
-                out=x_codes[chunk][:, g, :].bitcast(FP8X4),
-                scales=x_scales[chunk][:, g, :],
-                in_=x_grouped[chunk][:, g].rearrange("p n t -> p (n t)"),
+                out=x_codes[chunk][:].rearrange("p g n -> p (g n)").bitcast(FP8X4),
+                scales=x_scales[chunk][:].rearrange("p g n -> p (g n)"),
+                in_=x_grouped[chunk][:].rearrange("p g n t -> p (g n t)"),
             )
 
         def first_contraction(chunk):
-            width = chunks[chunk][2]
+            width, on_vector = CHUNKS[chunk][2:]
             z_scalar[chunk] = z_banks.tile([P, width], F32, name="z_scalar")
-            z_vector[chunk] = z_banks.tile([P, width], F32, name="z_vector")
-            for z_bank in (z_scalar[chunk], z_vector[chunk]):
+            targets = [z_scalar[chunk]]
+            if on_vector:
+                z_vector[chunk] = z_banks.tile([P, width], F32, name="z_vector")
+                targets.append(z_vector[chunk])
+            for z_bank in targets:
                 for g in range(IN_PASSES):
                     nc.tensor.matmul_mx(
                         out=z_bank[:],
@@ -156,9 +134,11 @@ def tile_rbfkanhead_kernel(
                         stop=(g == IN_PASSES - 1),
                     )
 
-        def squares_on_scalar(chunk):
-            squares[chunk] = work.tile([P, RBF_PASSES, chunks[chunk][2] // RUN, PACK, RUN], F32, name="squares")
-            for k in range(K_ON_SCALAR):
+        def squares_on_scalar(chunk, k_from, k_to):
+            width, on_vector = CHUNKS[chunk][2:]
+            if k_from == 0:
+                squares[chunk] = work.tile([P, RBF_PASSES, width // RUN, PACK, RUN], F32, name="squares")
+            for k in range(k_from, min(k_to, K - on_vector)):
                 nc.scalar.activation(
                     out=squares[chunk][:, k // PACK, :, k % PACK, :],
                     in_=z_scalar[chunk][:].rearrange("c (n i) -> c n i", i=RUN),
@@ -168,26 +148,31 @@ def tile_rbfkanhead_kernel(
                 )
 
         def squares_on_vector(chunk):
-            scaled = work.tile([P, K - K_ON_SCALAR, chunks[chunk][2]], F32, name="scaled")
-            for k in range(K_ON_SCALAR, K):
+            width, on_vector = CHUNKS[chunk][2:]
+            if not on_vector:
+                return
+            scaled[chunk] = work.tile([P, on_vector, width], F32, name="scaled")
+            for j in range(on_vector):
+                k = K - on_vector + j
                 nc.vector.tensor_scalar(
-                    out=scaled[:, k - K_ON_SCALAR, :],
+                    out=scaled[chunk][:, j, :],
                     in0=z_vector[chunk][:],
                     scalar1=shift[:, k : k + 1],
                     scalar2=inv_w[:, k : k + 1],
                     op0=ALU.add,
                     op1=ALU.mult,
                 )
-            for k in range(K_ON_SCALAR, K):
+            for j in range(on_vector):
+                k = K - on_vector + j
                 nc.vector.tensor_tensor(
                     out=squares[chunk][:, k // PACK, :, k % PACK, :],
-                    in0=scaled[:, k - K_ON_SCALAR, :].rearrange("c (n i) -> c n i", i=RUN),
-                    in1=scaled[:, k - K_ON_SCALAR, :].rearrange("c (n i) -> c n i", i=RUN),
+                    in0=scaled[chunk][:, j, :].rearrange("c (n i) -> c n i", i=RUN),
+                    in1=scaled[chunk][:, j, :].rearrange("c (n i) -> c n i", i=RUN),
                     op=ALU.mult,
                 )
 
         def exponentials(chunk, h):
-            width = chunks[chunk][2]
+            width = CHUNKS[chunk][2]
             if h == 0:
                 phi_grouped[chunk] = work.tile([P, RBF_PASSES, width, PACK], BF16, align_bytes=64, name="phi_grouped")
                 phi_codes[chunk] = work.tile([P, RBF_PASSES, width], U32, align_bytes=64, name="phi_codes")
@@ -206,9 +191,7 @@ def tile_rbfkanhead_kernel(
                 in_=phi_grouped[chunk][:, h].rearrange("c n t -> c (n t)"),
             )
             if h == 0:
-                out_ps[chunk] = [
-                    out_banks.tile([P, chunks[chunk][2]], F32, name="out_ps") for a in range(O_TILES)
-                ]
+                out_ps[chunk] = [out_banks.tile([P, CHUNKS[chunk][2]], F32, name="out_ps") for a in range(O_TILES)]
             for a in range(O_TILES):
                 nc.tensor.matmul_mx(
                     out=out_ps[chunk][a][:],
@@ -221,7 +204,7 @@ def tile_rbfkanhead_kernel(
                 )
 
         def bias_and_store(chunk, a, on_scalar=False):
-            image, first, width = chunks[chunk]
+            image, first, width, on_vector = CHUNKS[chunk]
             out_sb = stores.tile([P, width], F32, name="out_sb")
             if on_scalar:
                 nc.scalar.activation(
@@ -234,45 +217,82 @@ def tile_rbfkanhead_kernel(
             rows = out[image].rearrange("(a o) h w -> a o (h w)", o=P)
             nc.sync.dma_start(out=rows[a, :, first : first + width], in_=out_sb[:])
 
-        regroup_x(0)
+        tail = consts.tile([P, K], F32)
+        nc.scalar.activation(out=tail[:], in_=lw_bf[:], func=ACT.Abs)
+        nc.scalar.activation(out=tail[:], in_=tail[:], func=ACT.Exp, scale=-1.0)
+        nc.scalar.activation(out=tail[:], in_=tail[:], func=ACT.Ln, bias=ones[:, 0:1])
+        table_warmer = consts.tile([P, 1], F32)
+        nc.scalar.activation(out=table_warmer[:], in_=ones[:], func=ACT.Exp)
+
         for g in range(IN_PASSES):
-            quantise_x(0, g)
+            regroup_x(0, g)
+        widths = consts.tile([P, K], F32)
+        nc.vector.tensor_scalar(out=widths[:], in0=lw_bf[:], scalar1=0.0, scalar2=None, op0=ALU.max)
+        b_in_f = consts.tile([P, 1], F32)
+        nc.vector.tensor_copy(out=b_in_f[:], in_=b_in_bf[:])
+        shift = consts.tile([P, K], F32)
+        nc.vector.tensor_scalar(
+            out=shift[:], in0=centers_bf[:], scalar1=-1.0, scalar2=b_in_f[:, 0:1], op0=ALU.mult, op1=ALU.add
+        )
+        quantise_x(0)
         first_contraction(0)
+        out_bias_f = []
+        for a in range(O_TILES):
+            bias_f = consts.tile([P, 1], F32, name="out_bias_f%d" % a)
+            nc.vector.tensor_copy(out=bias_f[:], in_=out_bias_bf[a][:])
+            out_bias_f.append(bias_f)
+        nc.vector.tensor_tensor(out=widths[:], in0=widths[:], in1=tail[:], op=ALU.add)
+        nc.vector.tensor_scalar(out=widths[:], in0=widths[:], scalar1=1e-4, scalar2=None, op0=ALU.add)
+        inv_w = consts.tile([P, K], F32)
+        nc.vector.reciprocal(out=inv_w[:], in_=widths[:])
+        shift_w = consts.tile([P, K], F32)
+        nc.vector.tensor_tensor(out=shift_w[:], in0=shift[:], in1=inv_w[:], op=ALU.mult)
+        for g in range(IN_PASSES):
+            regroup_x(1, g)
 
         ow_grouped = consts.tile([P, O_TILES, RBF_PASSES, P, 2], F32, align_bytes=64)
-        for a in range(O_TILES):
-            ow_pairs = ow_raw[:, a, :].bitcast(F32)
-            ow_t = out_banks.tile([P, RBF_PASSES, 2, P], F32, name="ow_t", tag="out_ps")
-            for h in range(RBF_PASSES):
-                for u in range(2):
-                    nc.tensor.transpose(ow_t[:, h, u, :], ow_pairs[:, 2 * h + u : HID * K // 2 : 4], ident[:])
-            nc.vector.tensor_copy(out=ow_grouped[:, a], in_=ow_t[:].rearrange("c h u o -> c h o u"))
         ow_codes = consts.tile([P, O_TILES, RBF_PASSES, P], U32, align_bytes=64)
         ow_scales = consts.tile([P, O_TILES, RBF_PASSES, P], U8, align_bytes=64)
-        nc.vector.quantize_mx(
-            out=ow_codes[:].rearrange("c a h o -> c (a h o)").bitcast(FP8X4),
-            scales=ow_scales[:].rearrange("c a h o -> c (a h o)"),
-            in_=ow_grouped[:].rearrange("c a h o u -> c (a h o u)").bitcast(BF16),
-        )
+
+        def turn_out_weight():
+            for a in range(O_TILES):
+                ow_pairs = ow_raw[:, a, :].bitcast(F32)
+                ow_t = out_banks.tile([P, RBF_PASSES, 2, P], F32, name="ow_t", tag="out_ps")
+                for h in range(RBF_PASSES):
+                    for u in range(2):
+                        nc.tensor.transpose(ow_t[:, h, u, :], ow_pairs[:, 2 * h + u : HID * K // 2 : 4], ident[:])
+                nc.vector.tensor_copy(out=ow_grouped[:, a], in_=ow_t[:].rearrange("c h u o -> c h o u"))
+
+        def quantise_out_weight():
+            nc.vector.quantize_mx(
+                out=ow_codes[:].rearrange("c a h o -> c (a h o)").bitcast(FP8X4),
+                scales=ow_scales[:].rearrange("c a h o -> c (a h o)"),
+                in_=ow_grouped[:].rearrange("c a h o u -> c (a h o u)").bitcast(BF16),
+            )
 
         for chunk in range(n_chunks):
-            squares_on_scalar(chunk)
+            squares_on_scalar(chunk, 0, PACK)
             if chunk > 0:
                 second_contraction(chunk - 1, RBF_PASSES - 1)
-            squares_on_vector(chunk)
             if chunk + 1 < n_chunks:
-                regroup_x(chunk + 1)
-            for step in range(IN_PASSES):
-                if chunk + 1 < n_chunks:
-                    quantise_x(chunk + 1, step)
-                if chunk > 0:
-                    bias_and_store(chunk - 1, step)
-            if chunk + 1 < n_chunks:
+                quantise_x(chunk + 1)
                 first_contraction(chunk + 1)
-            for h in range(RBF_PASSES):
-                exponentials(chunk, h)
-                if h < RBF_PASSES - 1:
-                    second_contraction(chunk, h)
+            squares_on_vector(chunk)
+            exponentials(chunk, 0)
+            squares_on_scalar(chunk, PACK, K)
+            if chunk == 0:
+                turn_out_weight()
+            else:
+                for a in range(O_TILES):
+                    bias_and_store(chunk - 1, a)
+            if chunk + 2 < n_chunks:
+                regroup_x(chunk + 2, 0)
+            if chunk == 0:
+                quantise_out_weight()
+            second_contraction(chunk, 0)
+            if chunk + 2 < n_chunks:
+                regroup_x(chunk + 2, 1)
+            exponentials(chunk, 1)
         second_contraction(n_chunks - 1, RBF_PASSES - 1)
         bias_and_store(n_chunks - 1, 0)
         bias_and_store(n_chunks - 1, 1, on_scalar=True)

@@ -19,13 +19,14 @@ K_PASS = P * PACK
 IN_PASSES = C_IN // K_PASS
 RBF_PASSES = HID * K // K_PASS
 O_TILES = C_OUT // P
+TAIL = 256
 RUN = 4
 
 CHUNKS = (
     (0, 0, 512, 2),
     (0, 512, 512, 2),
     (1, 0, 512, 2),
-    (1, 512, 512, 2),
+    (1, 512, 512, 4),
 )
 
 FLOPS = 2 * B * HW * C_IN * HID + 2 * B * HW * HID * K * C_OUT
@@ -40,7 +41,7 @@ def tile_rbfkanhead_kernel(
         ctx.enter_context(tc.manual_schedule())
         consts = ctx.enter_context(tc.tile_pool(name="consts", bufs=1))
         work = ctx.enter_context(tc.tile_pool(name="work", bufs=2))
-        stores = ctx.enter_context(tc.tile_pool(name="stores", bufs=4))
+        stores = ctx.enter_context(tc.tile_pool(name="stores", bufs=8))
         z_banks = ctx.enter_context(tc.psum_pool(name="z_banks", bufs=2))
         out_banks = ctx.enter_context(tc.psum_pool(name="out_banks", bufs=4))
 
@@ -134,10 +135,13 @@ def tile_rbfkanhead_kernel(
                         stop=(g == IN_PASSES - 1),
                     )
 
+        def new_squares(chunk):
+            if chunk not in squares:
+                squares[chunk] = work.tile([P, RBF_PASSES, CHUNKS[chunk][2] // RUN, PACK, RUN], F32, name="squares")
+
         def squares_on_scalar(chunk, k_from, k_to):
-            width, on_vector = CHUNKS[chunk][2:]
-            if k_from == 0:
-                squares[chunk] = work.tile([P, RBF_PASSES, width // RUN, PACK, RUN], F32, name="squares")
+            on_vector = CHUNKS[chunk][3]
+            new_squares(chunk)
             for k in range(k_from, min(k_to, K - on_vector)):
                 nc.scalar.activation(
                     out=squares[chunk][:, k // PACK, :, k % PACK, :],
@@ -151,6 +155,7 @@ def tile_rbfkanhead_kernel(
             width, on_vector = CHUNKS[chunk][2:]
             if not on_vector:
                 return
+            new_squares(chunk)
             scaled[chunk] = work.tile([P, on_vector, width], F32, name="scaled")
             for j in range(on_vector):
                 k = K - on_vector + j
@@ -171,51 +176,65 @@ def tile_rbfkanhead_kernel(
                     op=ALU.mult,
                 )
 
-        def exponentials(chunk, h):
+        def exponentials(chunk, h, first=0, count=None):
             width = CHUNKS[chunk][2]
+            count = count or width
             if h == 0:
                 phi_grouped[chunk] = work.tile([P, RBF_PASSES, width, PACK], BF16, align_bytes=64, name="phi_grouped")
                 phi_codes[chunk] = work.tile([P, RBF_PASSES, width], U32, align_bytes=64, name="phi_codes")
                 phi_scales[chunk] = work.tile([P, RBF_PASSES, width], U8, align_bytes=64, name="phi_scales")
             nc.scalar.activation(
-                out=phi_grouped[chunk][:, h].rearrange("c (n i) t -> c n t i", i=RUN),
-                in_=squares[chunk][:, h],
+                out=phi_grouped[chunk][:, h, first : first + count].rearrange("c (n i) t -> c n t i", i=RUN),
+                in_=squares[chunk][:, h, first // RUN : (first + count) // RUN],
                 func=ACT.Exp,
                 scale=-1.0,
             )
 
-        def second_contraction(chunk, h):
+        def quantise_phi(chunk, h, first=0, count=None):
+            count = count or CHUNKS[chunk][2]
             nc.vector.quantize_mx(
-                out=phi_codes[chunk][:, h, :].bitcast(FP8X4),
-                scales=phi_scales[chunk][:, h, :],
-                in_=phi_grouped[chunk][:, h].rearrange("c n t -> c (n t)"),
+                out=phi_codes[chunk][:, h, first : first + count].bitcast(FP8X4),
+                scales=phi_scales[chunk][:, h, first : first + count],
+                in_=phi_grouped[chunk][:, h, first : first + count].rearrange("c n t -> c (n t)"),
             )
+
+        def multiply_phi(chunk, h, first=0, count=None):
+            count = count or CHUNKS[chunk][2]
             if h == 0:
-                out_ps[chunk] = [out_banks.tile([P, CHUNKS[chunk][2]], F32, name="out_ps") for a in range(O_TILES)]
+                out_ps[chunk, first] = [out_banks.tile([P, count], F32, name="out_ps") for a in range(O_TILES)]
             for a in range(O_TILES):
                 nc.tensor.matmul_mx(
-                    out=out_ps[chunk][a][:],
+                    out=out_ps[chunk, first][a][:],
                     lhsT=ow_codes[:, a, h, :].bitcast(FP8X4),
                     lhsT_scale=ow_scales[:, a, h, :],
-                    rhs=phi_codes[chunk][:, h, :].bitcast(FP8X4),
-                    rhs_scale=phi_scales[chunk][:, h, :],
+                    rhs=phi_codes[chunk][:, h, first : first + count].bitcast(FP8X4),
+                    rhs_scale=phi_scales[chunk][:, h, first : first + count],
                     start=(h == 0),
                     stop=(h == RBF_PASSES - 1),
                 )
 
-        def bias_and_store(chunk, a, on_scalar=False):
-            image, first, width, on_vector = CHUNKS[chunk]
-            out_sb = stores.tile([P, width], F32, name="out_sb")
+        def second_contraction(chunk, h):
+            quantise_phi(chunk, h)
+            multiply_phi(chunk, h)
+
+        def bias_and_store(chunk, a, first=0, count=None, on_scalar=False):
+            image, chunk_first, width, on_vector = CHUNKS[chunk]
+            count = count or width
+            out_sb = stores.tile([P, count], F32, name="out_sb")
             if on_scalar:
                 nc.scalar.activation(
-                    out=out_sb[:], in_=out_ps[chunk][a][:], func=ACT.Identity, bias=out_bias_f[a][:, 0:1]
+                    out=out_sb[:], in_=out_ps[chunk, first][a][:], func=ACT.Identity, bias=out_bias_f[a][:, 0:1]
                 )
             else:
                 nc.vector.tensor_scalar(
-                    out=out_sb[:], in0=out_ps[chunk][a][:], scalar1=out_bias_f[a][:, 0:1], scalar2=None, op0=ALU.add
+                    out=out_sb[:],
+                    in0=out_ps[chunk, first][a][:],
+                    scalar1=out_bias_f[a][:, 0:1],
+                    scalar2=None,
+                    op0=ALU.add,
                 )
             rows = out[image].rearrange("(a o) h w -> a o (h w)", o=P)
-            nc.sync.dma_start(out=rows[a, :, first : first + width], in_=out_sb[:])
+            nc.sync.dma_start(out=rows[a, :, chunk_first + first : chunk_first + first + count], in_=out_sb[:])
 
         tail = consts.tile([P, K], F32)
         nc.scalar.activation(out=tail[:], in_=lw_bf[:], func=ACT.Abs)
@@ -224,25 +243,26 @@ def tile_rbfkanhead_kernel(
         table_warmer = consts.tile([P, 1], F32)
         nc.scalar.activation(out=table_warmer[:], in_=ones[:], func=ACT.Exp)
 
-        for g in range(IN_PASSES):
-            regroup_x(0, g)
-        widths = consts.tile([P, K], F32)
-        nc.vector.tensor_scalar(out=widths[:], in0=lw_bf[:], scalar1=0.0, scalar2=None, op0=ALU.max)
+        floor_w = consts.tile([P, K], F32)
+        nc.gpsimd.tensor_scalar(out=floor_w[:], in0=lw_bf[:], scalar1=0.0, scalar2=1e-4, op0=ALU.max, op1=ALU.add)
         b_in_f = consts.tile([P, 1], F32)
-        nc.vector.tensor_copy(out=b_in_f[:], in_=b_in_bf[:])
+        nc.gpsimd.tensor_copy(out=b_in_f[:], in_=b_in_bf[:])
         shift = consts.tile([P, K], F32)
-        nc.vector.tensor_scalar(
+        nc.gpsimd.tensor_scalar(
             out=shift[:], in0=centers_bf[:], scalar1=-1.0, scalar2=b_in_f[:, 0:1], op0=ALU.mult, op1=ALU.add
         )
-        quantise_x(0)
-        first_contraction(0)
         out_bias_f = []
         for a in range(O_TILES):
             bias_f = consts.tile([P, 1], F32, name="out_bias_f%d" % a)
-            nc.vector.tensor_copy(out=bias_f[:], in_=out_bias_bf[a][:])
+            nc.gpsimd.tensor_copy(out=bias_f[:], in_=out_bias_bf[a][:])
             out_bias_f.append(bias_f)
-        nc.vector.tensor_tensor(out=widths[:], in0=widths[:], in1=tail[:], op=ALU.add)
-        nc.vector.tensor_scalar(out=widths[:], in0=widths[:], scalar1=1e-4, scalar2=None, op0=ALU.add)
+
+        for g in range(IN_PASSES):
+            regroup_x(0, g)
+        quantise_x(0)
+        first_contraction(0)
+        widths = consts.tile([P, K], F32)
+        nc.vector.tensor_tensor(out=widths[:], in0=floor_w[:], in1=tail[:], op=ALU.add)
         inv_w = consts.tile([P, K], F32)
         nc.vector.reciprocal(out=inv_w[:], in_=widths[:])
         shift_w = consts.tile([P, K], F32)
@@ -271,15 +291,20 @@ def tile_rbfkanhead_kernel(
             )
 
         for chunk in range(n_chunks):
+            last = chunk == n_chunks - 1
             squares_on_scalar(chunk, 0, PACK)
             if chunk > 0:
                 second_contraction(chunk - 1, RBF_PASSES - 1)
-            if chunk + 1 < n_chunks:
+            if not last:
                 quantise_x(chunk + 1)
                 first_contraction(chunk + 1)
-            squares_on_vector(chunk)
+                squares_on_vector(chunk)
             exponentials(chunk, 0)
             squares_on_scalar(chunk, PACK, K)
+            if last:
+                quantise_phi(chunk, 0)
+                for first in range(0, CHUNKS[chunk][2], TAIL):
+                    multiply_phi(chunk, 0, first, TAIL)
             if chunk == 0:
                 turn_out_weight()
             else:
@@ -289,10 +314,21 @@ def tile_rbfkanhead_kernel(
                 regroup_x(chunk + 2, 0)
             if chunk == 0:
                 quantise_out_weight()
-            second_contraction(chunk, 0)
+            if not last:
+                second_contraction(chunk, 0)
             if chunk + 2 < n_chunks:
                 regroup_x(chunk + 2, 1)
-            exponentials(chunk, 1)
-        second_contraction(n_chunks - 1, RBF_PASSES - 1)
-        bias_and_store(n_chunks - 1, 0)
-        bias_and_store(n_chunks - 1, 1, on_scalar=True)
+            if chunk == n_chunks - 2:
+                squares_on_vector(chunk + 1)
+            if not last:
+                exponentials(chunk, 1)
+        last = n_chunks - 1
+        ranges = list(range(0, CHUNKS[last][2], TAIL))
+        for first in ranges:
+            exponentials(last, 1, first, TAIL)
+        for first in ranges:
+            quantise_phi(last, 1, first, TAIL)
+            multiply_phi(last, 1, first, TAIL)
+        for first in ranges:
+            bias_and_store(last, 0, first, TAIL)
+            bias_and_store(last, 1, first, TAIL, on_scalar=True)

@@ -26,7 +26,7 @@ CHUNKS = (
     (0, 0, 512, 2),
     (0, 512, 512, 2),
     (1, 0, 512, 2),
-    (1, 512, 512, 4),
+    (1, 512, 512, 5),
 )
 
 FLOPS = 2 * B * HW * C_IN * HID + 2 * B * HW * HID * K * C_OUT
@@ -97,14 +97,24 @@ def tile_rbfkanhead_kernel(
         z_scalar, z_vector = {}, {}
         squares, scaled, phi_grouped, phi_codes, phi_scales, out_ps = {}, {}, {}, {}, {}, {}
 
-        def regroup_x(chunk, g):
+        def regroup_x(chunk, g, on_gpsimd=False):
             width = CHUNKS[chunk][2]
-            if g == 0:
-                x_grouped[chunk] = work.tile([P, IN_PASSES, width, PACK], BF16, align_bytes=64, name="x_grouped")
-            nc.vector.tensor_copy(
-                out=x_grouped[chunk][:, g].rearrange("p (n i) t -> p n t i", i=RUN),
-                in_=x_raws[chunk][:, g].rearrange("p t (n i) -> p n t i", i=RUN),
-            )
+            if chunk not in x_grouped:
+                x_grouped[chunk] = consts.tile([P, IN_PASSES, width, PACK], BF16, align_bytes=64, name="x_grouped")
+            if on_gpsimd:
+                nc.gpsimd.tensor_scalar(
+                    out=x_grouped[chunk][:, g],
+                    in0=x_raws[chunk][:, g].rearrange("p t n -> p n t"),
+                    scalar1=1.0,
+                    scalar2=0.0,
+                    op0=ALU.mult,
+                    op1=ALU.add,
+                )
+            else:
+                nc.vector.tensor_copy(
+                    out=x_grouped[chunk][:, g].rearrange("p (n i) t -> p n t i", i=RUN),
+                    in_=x_raws[chunk][:, g].rearrange("p t (n i) -> p n t i", i=RUN),
+                )
 
         def quantise_x(chunk):
             width = CHUNKS[chunk][2]
@@ -163,17 +173,19 @@ def tile_rbfkanhead_kernel(
                     out=scaled[chunk][:, j, :],
                     in0=z_vector[chunk][:],
                     scalar1=shift[:, k : k + 1],
-                    scalar2=inv_w[:, k : k + 1],
+                    scalar2=inv_w2[:, k : k + 1],
                     op0=ALU.add,
                     op1=ALU.mult,
                 )
             for j in range(on_vector):
                 k = K - on_vector + j
-                nc.vector.tensor_tensor(
+                nc.vector.scalar_tensor_tensor(
                     out=squares[chunk][:, k // PACK, :, k % PACK, :],
-                    in0=scaled[chunk][:, j, :].rearrange("c (n i) -> c n i", i=RUN),
+                    in0=z_vector[chunk][:].rearrange("c (n i) -> c n i", i=RUN),
+                    scalar=shift[:, k : k + 1],
                     in1=scaled[chunk][:, j, :].rearrange("c (n i) -> c n i", i=RUN),
-                    op=ALU.mult,
+                    op0=ALU.add,
+                    op1=ALU.mult,
                 )
 
         def exponentials(chunk, h, first=0, count=None):
@@ -267,6 +279,8 @@ def tile_rbfkanhead_kernel(
         nc.vector.reciprocal(out=inv_w[:], in_=widths[:])
         shift_w = consts.tile([P, K], F32)
         nc.vector.tensor_tensor(out=shift_w[:], in0=shift[:], in1=inv_w[:], op=ALU.mult)
+        inv_w2 = consts.tile([P, K], F32)
+        nc.gpsimd.tensor_tensor(out=inv_w2[:], in0=inv_w[:], in1=inv_w[:], op=ALU.mult)
         for g in range(IN_PASSES):
             regroup_x(1, g)
 
@@ -298,6 +312,8 @@ def tile_rbfkanhead_kernel(
             if not last:
                 quantise_x(chunk + 1)
                 first_contraction(chunk + 1)
+                if chunk + 2 < n_chunks:
+                    regroup_x(chunk + 2, 1, on_gpsimd=True)
                 squares_on_vector(chunk)
             exponentials(chunk, 0)
             squares_on_scalar(chunk, PACK, K)
@@ -316,8 +332,6 @@ def tile_rbfkanhead_kernel(
                 quantise_out_weight()
             if not last:
                 second_contraction(chunk, 0)
-            if chunk + 2 < n_chunks:
-                regroup_x(chunk + 2, 1)
             if chunk == n_chunks - 2:
                 squares_on_vector(chunk + 1)
             if not last:

@@ -306,7 +306,7 @@ def tile_rbfkanhead_kernel(
 
         for chunk in range(n_chunks):
             last = chunk == n_chunks - 1
-            squares_on_scalar(chunk, 0, PACK)
+            squares_on_scalar(chunk, 0, K)
             if chunk > 0:
                 second_contraction(chunk - 1, RBF_PASSES - 1)
             if not last:
@@ -316,7 +316,6 @@ def tile_rbfkanhead_kernel(
                     regroup_x(chunk + 2, 1, on_gpsimd=True)
                 squares_on_vector(chunk)
             exponentials(chunk, 0)
-            squares_on_scalar(chunk, PACK, K)
             if last:
                 quantise_phi(chunk, 0)
                 for first in range(0, CHUNKS[chunk][2], TAIL):

@@ -26,8 +26,9 @@ CHUNKS = (
     (0, 0, 512, 2),
     (0, 512, 512, 2),
     (1, 0, 512, 2),
-    (1, 512, 512, 5),
+    (1, 512, 512, 4),
 )
+ON_GPSIMD = (0, 0, 0, 2)
 
 FLOPS = 2 * B * HW * C_IN * HID + 2 * B * HW * HID * K * C_OUT
 
@@ -152,7 +153,7 @@ def tile_rbfkanhead_kernel(
         def squares_on_scalar(chunk, k_from, k_to):
             on_vector = CHUNKS[chunk][3]
             new_squares(chunk)
-            for k in range(k_from, min(k_to, K - on_vector)):
+            for k in range(k_from, min(k_to, K - on_vector - ON_GPSIMD[chunk])):
                 nc.scalar.activation(
                     out=squares[chunk][:, k // PACK, :, k % PACK, :],
                     in_=z_scalar[chunk][:].rearrange("c (n i) -> c n i", i=RUN),
@@ -168,7 +169,7 @@ def tile_rbfkanhead_kernel(
             new_squares(chunk)
             scaled[chunk] = work.tile([P, on_vector, width], F32, name="scaled")
             for j in range(on_vector):
-                k = K - on_vector + j
+                k = K - ON_GPSIMD[chunk] - on_vector + j
                 nc.vector.tensor_scalar(
                     out=scaled[chunk][:, j, :],
                     in0=z_vector[chunk][:],
@@ -178,7 +179,7 @@ def tile_rbfkanhead_kernel(
                     op1=ALU.mult,
                 )
             for j in range(on_vector):
-                k = K - on_vector + j
+                k = K - ON_GPSIMD[chunk] - on_vector + j
                 nc.vector.scalar_tensor_tensor(
                     out=squares[chunk][:, k // PACK, :, k % PACK, :],
                     in0=z_vector[chunk][:].rearrange("c (n i) -> c n i", i=RUN),
@@ -186,6 +187,31 @@ def tile_rbfkanhead_kernel(
                     in1=scaled[chunk][:, j, :].rearrange("c (n i) -> c n i", i=RUN),
                     op0=ALU.add,
                     op1=ALU.mult,
+                )
+
+        def squares_on_gpsimd(chunk):
+            width = CHUNKS[chunk][2]
+            new_squares(chunk)
+            z_sb = consts.tile([P, width], F32, name="z_sb")
+            nc.vector.tensor_copy(out=z_sb[:], in_=z_vector[chunk][:])
+            scaled_g = consts.tile([P, ON_GPSIMD[chunk], width], F32, name="scaled_g")
+            for j in range(ON_GPSIMD[chunk]):
+                k = K - ON_GPSIMD[chunk] + j
+                nc.gpsimd.tensor_scalar(
+                    out=scaled_g[:, j, :],
+                    in0=z_sb[:],
+                    scalar1=shift[:, k : k + 1],
+                    scalar2=inv_w[:, k : k + 1],
+                    op0=ALU.add,
+                    op1=ALU.mult,
+                )
+            for j in range(ON_GPSIMD[chunk]):
+                k = K - ON_GPSIMD[chunk] + j
+                nc.gpsimd.tensor_tensor(
+                    out=squares[chunk][:, k // PACK, :, k % PACK, :],
+                    in0=scaled_g[:, j, :].rearrange("c (n i) -> c n i", i=RUN),
+                    in1=scaled_g[:, j, :].rearrange("c (n i) -> c n i", i=RUN),
+                    op=ALU.mult,
                 )
 
         def exponentials(chunk, h, first=0, count=None):
@@ -320,6 +346,8 @@ def tile_rbfkanhead_kernel(
                 quantise_phi(chunk, 0)
                 for first in range(0, CHUNKS[chunk][2], TAIL):
                     multiply_phi(chunk, 0, first, TAIL)
+            if chunk == n_chunks - 2:
+                squares_on_gpsimd(chunk + 1)
             if chunk == 0:
                 turn_out_weight()
             else:
@@ -329,11 +357,10 @@ def tile_rbfkanhead_kernel(
                 regroup_x(chunk + 2, 0)
             if chunk == 0:
                 quantise_out_weight()
-            if not last:
-                second_contraction(chunk, 0)
             if chunk == n_chunks - 2:
                 squares_on_vector(chunk + 1)
             if not last:
+                second_contraction(chunk, 0)
                 exponentials(chunk, 1)
         last = n_chunks - 1
         ranges = list(range(0, CHUNKS[last][2], TAIL))

from contextlib import ExitStack

import concourse.mybir as mybir
from concourse.masks import make_identity

F32 = mybir.dt.float32
BF16 = mybir.dt.bfloat16
I32 = mybir.dt.int32
U32 = mybir.dt.uint32
U8 = mybir.dt.uint8
FP8X4 = mybir.dt.float8_e4m3fn_x4
ACT = mybir.ActivationFunctionType
ALU = mybir.AluOpType

B, C_IN, HW, HID, K, C_OUT = 2, 1024, 32 * 32, 128, 8, 256
P = 128
PACK = 4
K_PASS = P * PACK
IN_PASSES = C_IN // K_PASS
RBF_PASSES = HID * K // K_PASS
O_TILES = C_OUT // P
TAIL = 256
RUN = 4

CHUNKS = (
    (0, 0, 512, 2),
    (0, 512, 512, 2),
    (1, 0, 512, 2),
    (1, 512, 512, 4),
)
ON_GPSIMD = (0, 0, 0, 2)

FLOPS = 2 * B * HW * C_IN * HID + 2 * B * HW * HID * K * C_OUT


def tile_rbfkanhead_kernel(
    tc, x, w_in_words, w_in_scales, b_in, centers, log_widths, out_weight, out_bias, out
):
    nc = tc.nc
    n_chunks = len(CHUNKS)
    with ExitStack() as ctx:
        ctx.enter_context(tc.manual_schedule())
        consts = ctx.enter_context(tc.tile_pool(name="consts", bufs=1))
        work = ctx.enter_context(tc.tile_pool(name="work", bufs=2))
        stores = ctx.enter_context(tc.tile_pool(name="stores", bufs=8))
        z_banks = ctx.enter_context(tc.psum_pool(name="z_banks", bufs=2))
        out_banks = ctx.enter_context(tc.psum_pool(name="out_banks", bufs=4))

        def load_x(chunk):
            image, first, width, on_vector = CHUNKS[chunk]
            rows = x[image].rearrange("(g p t) h w -> g p t (h w)", p=P, t=PACK)
            x_raw = consts.tile([P, IN_PASSES, PACK, width], BF16, name="x_raw%d" % chunk)
            for g in range(IN_PASSES):
                nc.sync.dma_start(out=x_raw[:, g], in_=rows[g, :, :, first : first + width])
            return x_raw

        lw_bf = consts.tile([P, K], BF16)
        nc.scalar.dma_start(out=lw_bf[:], in_=log_widths[0, :, :, 0, 0])
        centers_bf = consts.tile([P, K], BF16)
        nc.scalar.dma_start(out=centers_bf[:], in_=centers[0, :, :, 0, 0])
        b_in_bf = consts.tile([P, 1], BF16)
        nc.scalar.dma_start(out=b_in_bf[:], in_=b_in.rearrange("(c one) -> c one", one=1))
        out_bias_bf = []
        for a in range(O_TILES):
            bias_bf = consts.tile([P, 1], BF16, name="out_bias_bf%d" % a)
            nc.scalar.dma_start(
                out=bias_bf[:], in_=out_bias[a * P : (a + 1) * P].rearrange("(o one) -> o one", one=1)
            )
            out_bias_bf.append(bias_bf)

        w_planes = consts.tile([P, IN_PASSES, HID], U8, align_bytes=64)
        nc.vector.memset(w_planes[:].bitcast(I32), 0)
        ones = consts.tile([P, 1], F32)
        nc.vector.memset(ones[:], 1.0)

        x_raws = [load_x(0)]
        w_words = consts.tile([P, IN_PASSES, HID], U32, align_bytes=64)
        for g in range(IN_PASSES):
            nc.sync.dma_start(
                out=w_words[:, g, :].bitcast(I32),
                in_=w_in_words[g].rearrange("p n t -> p (n t)").bitcast(I32),
            )
        for quadrant in range(4):
            nc.sync.dma_start(
                out=w_planes[32 * quadrant : 32 * quadrant + 4, :, :].bitcast(I32),
                in_=w_in_scales[:, 4 * quadrant : 4 * quadrant + 4, :].rearrange("g r n -> r g n").bitcast(I32),
            )
        x_raws.append(load_x(1))
        ow_raw = consts.tile([P, O_TILES, HID * K], BF16)
        nc.sync.dma_start(out=ow_raw[:], in_=out_weight.rearrange("(a o) c k -> o a (c k)", o=P))
        for chunk in range(2, n_chunks):
            x_raws.append(load_x(chunk))

        ident = consts.tile([P, P], F32)
        make_identity(nc, ident[:])

        x_grouped, x_codes, x_scales = {}, {}, {}
        z_scalar, z_vector = {}, {}
        squares, scaled, phi_grouped, phi_codes, phi_scales, out_ps = {}, {}, {}, {}, {}, {}

        def regroup_x(chunk, g, on_gpsimd=False):
            width = CHUNKS[chunk][2]
            if chunk not in x_grouped:
                x_grouped[chunk] = consts.tile([P, IN_PASSES, width, PACK], BF16, align_bytes=64, name="x_grouped")
            if on_gpsimd:
                nc.gpsimd.tensor_scalar(
                    out=x_grouped[chunk][:, g],
                    in0=x_raws[chunk][:, g].rearrange("p t n -> p n t"),
                    scalar1=1.0,
                    scalar2=0.0,
                    op0=ALU.mult,
                    op1=ALU.add,
                )
            else:
                nc.vector.tensor_copy(
                    out=x_grouped[chunk][:, g].rearrange("p (n i) t -> p n t i", i=RUN),
                    in_=x_raws[chunk][:, g].rearrange("p t (n i) -> p n t i", i=RUN),
                )

        def quantise_x(chunk):
            width = CHUNKS[chunk][2]
            x_codes[chunk] = consts.tile([P, IN_PASSES, width], U32, align_bytes=64, name="x_codes%d" % chunk)
            x_scales[chunk] = consts.tile([P, IN_PASSES, width], U8, align_bytes=64, name="x_scales%d" % chunk)
            nc.vector.quantize_mx(
                out=x_codes[chunk][:].rearrange("p g n -> p (g n)").bitcast(FP8X4),
                scales=x_scales[chunk][:].rearrange("p g n -> p (g n)"),
                in_=x_grouped[chunk][:].rearrange("p g n t -> p (g n t)"),
            )

        def first_contraction(chunk):
            width, on_vector = CHUNKS[chunk][2:]
            z_scalar[chunk] = z_banks.tile([P, width], F32, name="z_scalar")
            targets = [z_scalar[chunk]]
            if on_vector:
                z_vector[chunk] = z_banks.tile([P, width], F32, name="z_vector")
                targets.append(z_vector[chunk])
            for z_bank in targets:
                for g in range(IN_PASSES):
                    nc.tensor.matmul_mx(
                        out=z_bank[:],
                        lhsT=w_words[:, g, :].bitcast(FP8X4),
                        lhsT_scale=w_planes[:, g, :],
                        rhs=x_codes[chunk][:, g, :].bitcast(FP8X4),
                        rhs_scale=x_scales[chunk][:, g, :],
                        start=(g == 0),
                        stop=(g == IN_PASSES - 1),
                    )

        def new_squares(chunk):
            if chunk not in squares:
                squares[chunk] = work.tile([P, RBF_PASSES, CHUNKS[chunk][2] // RUN, PACK, RUN], F32, name="squares")

        def squares_on_scalar(chunk, k_from, k_to):
            on_vector = CHUNKS[chunk][3]
            new_squares(chunk)
            for k in range(k_from, min(k_to, K - on_vector - ON_GPSIMD[chunk])):
                nc.scalar.activation(
                    out=squares[chunk][:, k // PACK, :, k % PACK, :],
                    in_=z_scalar[chunk][:].rearrange("c (n i) -> c n i", i=RUN),
                    func=ACT.Square,
                    scale=inv_w[:, k : k + 1],
                    bias=shift_w[:, k : k + 1],
                )

        def squares_on_vector(chunk):
            width, on_vector = CHUNKS[chunk][2:]
            if not on_vector:
                return
            new_squares(chunk)
            scaled[chunk] = work.tile([P, on_vector, width], F32, name="scaled")
            for j in range(on_vector):
                k = K - ON_GPSIMD[chunk] - on_vector + j
                nc.vector.tensor_scalar(
                    out=scaled[chunk][:, j, :],
                    in0=z_vector[chunk][:],
                    scalar1=shift[:, k : k + 1],
                    scalar2=inv_w2[:, k : k + 1],
                    op0=ALU.add,
                    op1=ALU.mult,
                )
            for j in range(on_vector):
                k = K - ON_GPSIMD[chunk] - on_vector + j
                nc.vector.scalar_tensor_tensor(
                    out=squares[chunk][:, k // PACK, :, k % PACK, :],
                    in0=z_vector[chunk][:].rearrange("c (n i) -> c n i", i=RUN),
                    scalar=shift[:, k : k + 1],
                    in1=scaled[chunk][:, j, :].rearrange("c (n i) -> c n i", i=RUN),
                    op0=ALU.add,
                    op1=ALU.mult,
                )

        def squares_on_gpsimd(chunk):
            width = CHUNKS[chunk][2]
            new_squares(chunk)
            z_sb = consts.tile([P, width], F32, name="z_sb")
            nc.vector.tensor_copy(out=z_sb[:], in_=z_vector[chunk][:])
            scaled_g = consts.tile([P, ON_GPSIMD[chunk], width], F32, name="scaled_g")
            for j in range(ON_GPSIMD[chunk]):
                k = K - ON_GPSIMD[chunk] + j
                nc.gpsimd.tensor_scalar(
                    out=scaled_g[:, j, :],
                    in0=z_sb[:],
                    scalar1=shift[:, k : k + 1],
                    scalar2=inv_w[:, k : k + 1],
                    op0=ALU.add,
                    op1=ALU.mult,
                )
            for j in range(ON_GPSIMD[chunk]):
                k = K - ON_GPSIMD[chunk] + j
                nc.gpsimd.tensor_tensor(
                    out=squares[chunk][:, k // PACK, :, k % PACK, :],
                    in0=scaled_g[:, j, :].rearrange("c (n i) -> c n i", i=RUN),
                    in1=scaled_g[:, j, :].rearrange("c (n i) -> c n i", i=RUN),
                    op=ALU.mult,
                )

        def exponentials(chunk, h, first=0, count=None):
            width = CHUNKS[chunk][2]
            count = count or width
            if h == 0:
                phi_grouped[chunk] = work.tile([P, RBF_PASSES, width, PACK], BF16, align_bytes=64, name="phi_grouped")
                phi_codes[chunk] = work.tile([P, RBF_PASSES, width], U32, align_bytes=64, name="phi_codes")
                phi_scales[chunk] = work.tile([P, RBF_PASSES, width], U8, align_bytes=64, name="phi_scales")
            nc.scalar.activation(
                out=phi_grouped[chunk][:, h, first : first + count].rearrange("c (n i) t -> c n t i", i=RUN),
                in_=squares[chunk][:, h, first // RUN : (first + count) // RUN],
                func=ACT.Exp,
                scale=-1.0,
            )

        def quantise_phi(chunk, h, first=0, count=None):
            count = count or CHUNKS[chunk][2]
            nc.vector.quantize_mx(
                out=phi_codes[chunk][:, h, first : first + count].bitcast(FP8X4),
                scales=phi_scales[chunk][:, h, first : first + count],
                in_=phi_grouped[chunk][:, h, first : first + count].rearrange("c n t -> c (n t)"),
            )

        def multiply_phi(chunk, h, first=0, count=None):
            count = count or CHUNKS[chunk][2]
            if h == 0:
                out_ps[chunk, first] = [out_banks.tile([P, count], F32, name="out_ps") for a in range(O_TILES)]
            for a in range(O_TILES):
                nc.tensor.matmul_mx(
                    out=out_ps[chunk, first][a][:],
                    lhsT=ow_codes[:, a, h, :].bitcast(FP8X4),
                    lhsT_scale=ow_scales[:, a, h, :],
                    rhs=phi_codes[chunk][:, h, first : first + count].bitcast(FP8X4),
                    rhs_scale=phi_scales[chunk][:, h, first : first + count],
                    start=(h == 0),
                    stop=(h == RBF_PASSES - 1),
                )

        def second_contraction(chunk, h):
            quantise_phi(chunk, h)
            multiply_phi(chunk, h)

        def bias_and_store(chunk, a, first=0, count=None, on_scalar=False):
            image, chunk_first, width, on_vector = CHUNKS[chunk]
            count = count or width
            out_sb = stores.tile([P, count], F32, name="out_sb")
            if on_scalar:
                nc.scalar.activation(
                    out=out_sb[:], in_=out_ps[chunk, first][a][:], func=ACT.Identity, bias=out_bias_f[a][:, 0:1]
                )
            else:
                nc.vector.tensor_scalar(
                    out=out_sb[:],
                    in0=out_ps[chunk, first][a][:],
                    scalar1=out_bias_f[a][:, 0:1],
                    scalar2=None,
                    op0=ALU.add,
                )
            rows = out[image].rearrange("(a o) h w -> a o (h w)", o=P)
            nc.sync.dma_start(out=rows[a, :, chunk_first + first : chunk_first + first + count], in_=out_sb[:])

        tail = consts.tile([P, K], F32)
        nc.scalar.activation(out=tail[:], in_=lw_bf[:], func=ACT.Abs)
        nc.scalar.activation(out=tail[:], in_=tail[:], func=ACT.Exp, scale=-1.0)
        nc.scalar.activation(out=tail[:], in_=tail[:], func=ACT.Ln, bias=ones[:, 0:1])
        table_warmer = consts.tile([P, 1], F32)
        nc.scalar.activation(out=table_warmer[:], in_=ones[:], func=ACT.Exp)

        floor_w = consts.tile([P, K], F32)
        nc.gpsimd.tensor_scalar(out=floor_w[:], in0=lw_bf[:], scalar1=0.0, scalar2=1e-4, op0=ALU.max, op1=ALU.add)
        b_in_f = consts.tile([P, 1], F32)
        nc.gpsimd.tensor_copy(out=b_in_f[:], in_=b_in_bf[:])
        shift = consts.tile([P, K], F32)
        nc.gpsimd.tensor_scalar(
            out=shift[:], in0=centers_bf[:], scalar1=-1.0, scalar2=b_in_f[:, 0:1], op0=ALU.mult, op1=ALU.add
        )
        out_bias_f = []
        for a in range(O_TILES):
            bias_f = consts.tile([P, 1], F32, name="out_bias_f%d" % a)
            nc.gpsimd.tensor_copy(out=bias_f[:], in_=out_bias_bf[a][:])
            out_bias_f.append(bias_f)

        for g in range(IN_PASSES):
            regroup_x(0, g)
        quantise_x(0)
        first_contraction(0)
        widths = consts.tile([P, K], F32)
        nc.vector.tensor_tensor(out=widths[:], in0=floor_w[:], in1=tail[:], op=ALU.add)
        inv_w = consts.tile([P, K], F32)
        nc.vector.reciprocal(out=inv_w[:], in_=widths[:])
        shift_w = consts.tile([P, K], F32)
        nc.vector.tensor_tensor(out=shift_w[:], in0=shift[:], in1=inv_w[:], op=ALU.mult)
        inv_w2 = consts.tile([P, K], F32)
        nc.gpsimd.tensor_tensor(out=inv_w2[:], in0=inv_w[:], in1=inv_w[:], op=ALU.mult)
        for g in range(IN_PASSES):
            regroup_x(1, g)

        ow_grouped = consts.tile([P, O_TILES, RBF_PASSES, P, 2], F32, align_bytes=64)
        ow_codes = consts.tile([P, O_TILES, RBF_PASSES, P], U32, align_bytes=64)
        ow_scales = consts.tile([P, O_TILES, RBF_PASSES, P], U8, align_bytes=64)

        def turn_out_weight():
            for a in range(O_TILES):
                ow_pairs = ow_raw[:, a, :].bitcast(F32)
                ow_t = out_banks.tile([P, RBF_PASSES, 2, P], F32, name="ow_t", tag="out_ps")
                for h in range(RBF_PASSES):
                    for u in range(2):
                        nc.tensor.transpose(ow_t[:, h, u, :], ow_pairs[:, 2 * h + u : HID * K // 2 : 4], ident[:])
                nc.vector.tensor_copy(out=ow_grouped[:, a], in_=ow_t[:].rearrange("c h u o -> c h o u"))

        def quantise_out_weight():
            nc.vector.quantize_mx(
                out=ow_codes[:].rearrange("c a h o -> c (a h o)").bitcast(FP8X4),
                scales=ow_scales[:].rearrange("c a h o -> c (a h o)"),
                in_=ow_grouped[:].rearrange("c a h o u -> c (a h o u)").bitcast(BF16),
            )

        for chunk in range(n_chunks):
            last = chunk == n_chunks - 1
            squares_on_scalar(chunk, 0, K)
            if chunk > 0:
                second_contraction(chunk - 1, RBF_PASSES - 1)
            if not last:
                quantise_x(chunk + 1)
                first_contraction(chunk + 1)
                if chunk + 2 < n_chunks:
                    regroup_x(chunk + 2, 1, on_gpsimd=True)
                squares_on_vector(chunk)
            exponentials(chunk, 0)
            if last:
                quantise_phi(chunk, 0)
                for first in range(0, CHUNKS[chunk][2], TAIL):
                    multiply_phi(chunk, 0, first, TAIL)
            if chunk == n_chunks - 2:
                squares_on_gpsimd(chunk + 1)
            if chunk == 0:
                turn_out_weight()
            else:
                for a in range(O_TILES):
                    bias_and_store(chunk - 1, a)
            if chunk + 2 < n_chunks:
                regroup_x(chunk + 2, 0)
            if chunk == 0:
                quantise_out_weight()
            if chunk == n_chunks - 2:
                squares_on_vector(chunk + 1)
            if not last:
                second_contraction(chunk, 0)
                exponentials(chunk, 1)
        last = n_chunks - 1
        ranges = list(range(0, CHUNKS[last][2], TAIL))
        for first in ranges:
            exponentials(last, 1, first, TAIL)
        for first in ranges:
            quantise_phi(last, 1, first, TAIL)
            multiply_phi(last, 1, first, TAIL)
        for first in ranges:
            bias_and_store(last, 0, first, TAIL)
            bias_and_store(last, 1, first, TAIL, on_scalar=True)
